import numpy as np
import ml_dtypes

BF16 = ml_dtypes.bfloat16


def bf(x):
    return np.asarray(x, np.float32).astype(BF16)


def f32(x):
    return np.asarray(x, np.float32)


def f64(x):
    return np.asarray(x).astype(np.float64)


def striped(idx):
    return np.tile(idx.reshape(-1, 16).T, (8, 1))


C, S, N = 256, 4096, 2048
LO, HI = -5.0, 3.0


def setup_inputs():
    return {"x_store": f32(np.random.standard_normal((C, S))), "x_masked": bf(np.random.standard_normal((C, N))), "w_scale": bf(np.random.standard_normal((C, C)) / np.sqrt(C)), "b_scale": f32(0.1 * np.random.standard_normal((C, 1))), "w_shift": bf(np.random.standard_normal((C, C)) / np.sqrt(C)), "b_shift": f32(0.1 * np.random.standard_normal((C, 1))), "offs": striped(np.random.permutation(np.tile(np.arange(S), 2))[:N])}


def reference(x_store, x_masked, w_scale, b_scale, w_shift, b_shift, offs):
    idx = offs[:16].T.reshape(-1)
    log_scale = f64(w_scale).T @ f64(x_masked) + f64(b_scale)
    shift = f64(w_shift).T @ f64(x_masked) + f64(b_shift)
    scale = np.exp(np.minimum(np.maximum(log_scale, LO), HI))
    return f64(x_store)[:, idx] * scale + shift

@@ -1,0 +1,85 @@
+import math
+
+import concourse.mybir as mybir
+
+F32 = mybir.dt.float32
+BF16 = mybir.dt.bfloat16
+U16 = mybir.dt.uint16
+ALU = mybir.AluOpType
+ACT = mybir.ActivationFunctionType
+
+P = 128
+C, S, N = 256, 4096, 2048
+BLOCKS = C // P
+PIECE = 512
+PIECES = N // PIECE
+LO, HI = -5.0, 3.0
+
+FLOPS = 2 * 2 * C * C * N
+
+
+def tile_maskedcouplingaffine_kernel(
+    tc, x_store, x_masked, w_scale, b_scale, w_shift, b_shift, offs, out
+):
+    nc = tc.nc
+    with (
+        tc.tile_pool(name="held", bufs=1) as held,
+        tc.tile_pool(name="work", bufs=4) as work,
+        tc.psum_pool(name="psum", bufs=4) as psum,
+    ):
+        offsets = held.tile([P, N // 16], U16, name="offsets")
+        nc.sync.dma_start(offsets[:], offs)
+        weights_scale, weights_shift, masked, store = [], [], [], []
+        for k in range(BLOCKS):
+            rows = slice(k * P, (k + 1) * P)
+            weights_scale.append(held.tile([P, C], BF16, name=f"weights_scale{k}"))
+            nc.sync.dma_start(weights_scale[k][:], w_scale[rows, :])
+            weights_shift.append(held.tile([P, C], BF16, name=f"weights_shift{k}"))
+            nc.sync.dma_start(weights_shift[k][:], w_shift[rows, :])
+            masked.append(held.tile([P, N], BF16, name=f"masked{k}"))
+            nc.sync.dma_start(masked[k][:], x_masked[rows, :])
+        for c in range(BLOCKS):
+            store.append(held.tile([P, S], F32, name=f"store{c}"))
+            nc.sync.dma_start(store[c][:], x_store[c * P : (c + 1) * P, :])
+        bias_scale, bias_shift = [], []
+        for c in range(BLOCKS):
+            rows = slice(c * P, (c + 1) * P)
+            bias_scale.append(held.tile([P, 1], F32, name=f"bias_scale{c}"))
+            nc.scalar.dma_start(bias_scale[c][:], b_scale[rows, :])
+            bias_shift.append(held.tile([P, 1], F32, name=f"bias_shift{c}"))
+            nc.scalar.dma_start(bias_shift[c][:], b_shift[rows, :])
+
+        for c in range(BLOCKS):
+            features = slice(c * P, (c + 1) * P)
+            for piece in range(PIECES):
+                columns = slice(piece * PIECE, (piece + 1) * PIECE)
+
+                log_scale = psum.tile([P, PIECE], F32, name="log_scale")
+                shift = psum.tile([P, PIECE], F32, name="shift")
+                for k in range(BLOCKS):
+                    nc.tensor.matmul(
+                        log_scale[:], weights_scale[k][:, features], masked[k][:, columns],
+                        start=(k == 0), stop=(k == BLOCKS - 1),
+                    )
+                for k in range(BLOCKS):
+                    nc.tensor.matmul(
+                        shift[:], weights_shift[k][:, features], masked[k][:, columns],
+                        start=(k == 0), stop=(k == BLOCKS - 1),
+                    )
+
+                unclipped = work.tile([P, PIECE], F32, name="unclipped")
+                nc.scalar.activation(unclipped[:], log_scale[:], ACT.Exp, bias=bias_scale[c][:])
+                scale = work.tile([P, PIECE], F32, name="scale")
+                nc.vector.tensor_scalar(
+                    scale[:], unclipped[:], math.exp(LO), math.exp(HI), ALU.max, ALU.min
+                )
+
+                picked = store[c][:].indirect(offsets[:, piece * (PIECE // 16) : (piece + 1) * (PIECE // 16)])
+                scaled = work.tile([P, PIECE], F32, name="scaled")
+                nc.vector.tensor_tensor(scaled[:], picked, scale[:], ALU.mult)
+
+                result = work.tile([P, PIECE], F32, name="result")
+                nc.vector.scalar_tensor_tensor(
+                    result[:], shift[:], bias_shift[c][:], scaled[:], ALU.add, ALU.add
+                )
+                nc.sync.dma_start(out[features, columns], result[:])

@@ -24,20 +24,20 @@ def tile_maskedcouplingaffine_kernel(
     nc = tc.nc
     with (
         tc.tile_pool(name="held", bufs=1) as held,
-        tc.tile_pool(name="work", bufs=4) as work,
         tc.psum_pool(name="psum", bufs=4) as psum,
     ):
         offsets = held.tile([P, N // 16], U16, name="offsets")
         nc.sync.dma_start(offsets[:], offs)
-        weights_scale, weights_shift, masked, store = [], [], [], []
-        for k in range(BLOCKS):
-            rows = slice(k * P, (k + 1) * P)
-            weights_scale.append(held.tile([P, C], BF16, name=f"weights_scale{k}"))
-            nc.sync.dma_start(weights_scale[k][:], w_scale[rows, :])
-            weights_shift.append(held.tile([P, C], BF16, name=f"weights_shift{k}"))
-            nc.sync.dma_start(weights_shift[k][:], w_shift[rows, :])
-            masked.append(held.tile([P, N], BF16, name=f"masked{k}"))
-            nc.sync.dma_start(masked[k][:], x_masked[rows, :])
+        weights_scale = held.tile([P, BLOCKS, C], BF16, name="weights_scale")
+        nc.sync.dma_start(weights_scale[:], w_scale.rearrange("(k p) c -> p k c", p=P))
+        masked = held.tile([P, BLOCKS, N], BF16, name="masked")
+        masked_dram = x_masked.rearrange("(k p) n -> p k n", p=P)
+        for half in range(2):
+            columns = slice(half * (N // 2), (half + 1) * (N // 2))
+            nc.sync.dma_start(masked[:, :, columns], masked_dram[:, :, columns])
+        weights_shift = held.tile([P, BLOCKS, C], BF16, name="weights_shift")
+        nc.sync.dma_start(weights_shift[:], w_shift.rearrange("(k p) c -> p k c", p=P))
+        store = []
         for c in range(BLOCKS):
             store.append(held.tile([P, S], F32, name=f"store{c}"))
             nc.sync.dma_start(store[c][:], x_store[c * P : (c + 1) * P, :])
@@ -45,41 +45,48 @@ def tile_maskedcouplingaffine_kernel(
         for c in range(BLOCKS):
             rows = slice(c * P, (c + 1) * P)
             bias_scale.append(held.tile([P, 1], F32, name=f"bias_scale{c}"))
-            nc.scalar.dma_start(bias_scale[c][:], b_scale[rows, :])
+            nc.gpsimd.dma_start(bias_scale[c][:], b_scale[rows, :])
             bias_shift.append(held.tile([P, 1], F32, name=f"bias_shift{c}"))
-            nc.scalar.dma_start(bias_shift[c][:], b_shift[rows, :])
+            nc.gpsimd.dma_start(bias_shift[c][:], b_shift[rows, :])
 
+        def product(name, weights, c, piece):
+            bank = psum.tile([P, PIECE], F32, name=name)
+            for k in range(BLOCKS):
+                nc.tensor.matmul(
+                    bank[:],
+                    weights[:, k, c * P : (c + 1) * P],
+                    masked[:, k, piece * PIECE : (piece + 1) * PIECE],
+                    start=(k == 0),
+                    stop=(k == BLOCKS - 1),
+                )
+            return bank
+
+        scale = []
         for c in range(BLOCKS):
-            features = slice(c * P, (c + 1) * P)
+            unclipped = held.tile([P, N], F32, name=f"unclipped{c}")
+            scale.append(held.tile([P, N], F32, name=f"scale{c}"))
             for piece in range(PIECES):
                 columns = slice(piece * PIECE, (piece + 1) * PIECE)
-
-                log_scale = psum.tile([P, PIECE], F32, name="log_scale")
-                shift = psum.tile([P, PIECE], F32, name="shift")
-                for k in range(BLOCKS):
-                    nc.tensor.matmul(
-                        log_scale[:], weights_scale[k][:, features], masked[k][:, columns],
-                        start=(k == 0), stop=(k == BLOCKS - 1),
-                    )
-                for k in range(BLOCKS):
-                    nc.tensor.matmul(
-                        shift[:], weights_shift[k][:, features], masked[k][:, columns],
-                        start=(k == 0), stop=(k == BLOCKS - 1),
-                    )
-
-                unclipped = work.tile([P, PIECE], F32, name="unclipped")
-                nc.scalar.activation(unclipped[:], log_scale[:], ACT.Exp, bias=bias_scale[c][:])
-                scale = work.tile([P, PIECE], F32, name="scale")
+                log_scale = product("log_scale", weights_scale, c, piece)
+                nc.scalar.activation(unclipped[:, columns], log_scale[:], ACT.Exp, bias=bias_scale[c][:])
                 nc.vector.tensor_scalar(
-                    scale[:], unclipped[:], math.exp(LO), math.exp(HI), ALU.max, ALU.min
+                    scale[c][:, columns], unclipped[:, columns], math.exp(LO), math.exp(HI), ALU.max, ALU.min
                 )
 
+        shift = []
+        for c in range(BLOCKS):
+            shift.append(held.tile([P, N], F32, name=f"shift{c}"))
+            for piece in range(PIECES):
+                columns = slice(piece * PIECE, (piece + 1) * PIECE)
+                unbiased = product("unbiased", weights_shift, c, piece)
+                nc.scalar.activation(shift[c][:, columns], unbiased[:], ACT.Identity, bias=bias_shift[c][:])
+
+        for c in range(BLOCKS):
+            scaled = held.tile([P, N], F32, name=f"scaled{c}")
+            result = held.tile([P, N], F32, name=f"result{c}")
+            for piece in range(PIECES):
+                columns = slice(piece * PIECE, (piece + 1) * PIECE)
                 picked = store[c][:].indirect(offsets[:, piece * (PIECE // 16) : (piece + 1) * (PIECE // 16)])
-                scaled = work.tile([P, PIECE], F32, name="scaled")
-                nc.vector.tensor_tensor(scaled[:], picked, scale[:], ALU.mult)
-
-                result = work.tile([P, PIECE], F32, name="result")
-                nc.vector.scalar_tensor_tensor(
-                    result[:], shift[:], bias_shift[c][:], scaled[:], ALU.add, ALU.add
-                )
-                nc.sync.dma_start(out[features, columns], result[:])
+                nc.vector.tensor_tensor(scaled[:, columns], picked, scale[c][:, columns], ALU.mult)
+                nc.gpsimd.tensor_tensor(result[:, columns], scaled[:, columns], shift[c][:, columns], ALU.add)
+                nc.sync.dma_start(out[c * P : (c + 1) * P, columns], result[:, columns])

@@ -24,8 +24,12 @@ def tile_maskedcouplingaffine_kernel(
     nc = tc.nc
     with (
         tc.tile_pool(name="held", bufs=1) as held,
-        tc.psum_pool(name="psum", bufs=4) as psum,
+        tc.psum_pool(name="psum_bias", bufs=1) as psum_bias,
+        tc.psum_pool(name="psum", bufs=7) as psum,
     ):
+        bias_rows = held.tile([1, 2 * C], F32, name="bias_rows")
+        nc.sync.dma_start(bias_rows[:, 0:C], b_scale.rearrange("c one -> one c"))
+        nc.sync.dma_start(bias_rows[:, C : 2 * C], b_shift.rearrange("c one -> one c"))
         offsets = held.tile([P, N // 16], U16, name="offsets")
         nc.sync.dma_start(offsets[:], offs)
         weights_scale = held.tile([P, BLOCKS, C], BF16, name="weights_scale")
@@ -35,22 +39,26 @@ def tile_maskedcouplingaffine_kernel(
         for half in range(2):
             columns = slice(half * (N // 2), (half + 1) * (N // 2))
             nc.sync.dma_start(masked[:, :, columns], masked_dram[:, :, columns])
+        store = [held.tile([P, S], F32, name=f"store{c}") for c in range(BLOCKS)]
+        nc.sync.dma_start(store[0][:], x_store[0:P, :])
         weights_shift = held.tile([P, BLOCKS, C], BF16, name="weights_shift")
         nc.sync.dma_start(weights_shift[:], w_shift.rearrange("(k p) c -> p k c", p=P))
-        store = []
-        for c in range(BLOCKS):
-            store.append(held.tile([P, S], F32, name=f"store{c}"))
-            nc.sync.dma_start(store[c][:], x_store[c * P : (c + 1) * P, :])
-        bias_scale, bias_shift = [], []
-        for c in range(BLOCKS):
-            rows = slice(c * P, (c + 1) * P)
-            bias_scale.append(held.tile([P, 1], F32, name=f"bias_scale{c}"))
-            nc.gpsimd.dma_start(bias_scale[c][:], b_scale[rows, :])
-            bias_shift.append(held.tile([P, 1], F32, name=f"bias_shift{c}"))
-            nc.gpsimd.dma_start(bias_shift[c][:], b_shift[rows, :])
+        nc.sync.dma_start(store[1][:], x_store[P : 2 * P, :])
 
-        def product(name, weights, c, piece):
-            bank = psum.tile([P, PIECE], F32, name=name)
+        one = held.tile([1, 1], F32, name="one")
+        nc.vector.memset(one[:], 1.0)
+        bias_bank = psum_bias.tile([P, 2 * BLOCKS], F32, name="bias_bank")
+        for i in range(2 * BLOCKS):
+            nc.tensor.matmul(
+                bias_bank[:, i : i + 1], bias_rows[:, i * P : (i + 1) * P], one[:], start=True, stop=True
+            )
+        biases = held.tile([P, 2 * BLOCKS], F32, name="biases")
+        nc.vector.tensor_copy(biases[:], bias_bank[:])
+        bias_scale = [biases[:, c : c + 1] for c in range(BLOCKS)]
+        bias_shift = [biases[:, BLOCKS + c : BLOCKS + c + 1] for c in range(BLOCKS)]
+
+        def product(weights, c, piece):
+            bank = psum.tile([P, PIECE], F32, name="bank")
             for k in range(BLOCKS):
                 nc.tensor.matmul(
                     bank[:],
@@ -67,8 +75,8 @@ def tile_maskedcouplingaffine_kernel(
             scale.append(held.tile([P, N], F32, name=f"scale{c}"))
             for piece in range(PIECES):
                 columns = slice(piece * PIECE, (piece + 1) * PIECE)
-                log_scale = product("log_scale", weights_scale, c, piece)
-                nc.scalar.activation(unclipped[:, columns], log_scale[:], ACT.Exp, bias=bias_scale[c][:])
+                log_scale = product(weights_scale, c, piece)
+                nc.scalar.activation(unclipped[:, columns], log_scale[:], ACT.Exp, bias=bias_scale[c])
                 nc.vector.tensor_scalar(
                     scale[c][:, columns], unclipped[:, columns], math.exp(LO), math.exp(HI), ALU.max, ALU.min
                 )
@@ -78,8 +86,8 @@ def tile_maskedcouplingaffine_kernel(
             shift.append(held.tile([P, N], F32, name=f"shift{c}"))
             for piece in range(PIECES):
                 columns = slice(piece * PIECE, (piece + 1) * PIECE)
-                unbiased = product("unbiased", weights_shift, c, piece)
-                nc.scalar.activation(shift[c][:, columns], unbiased[:], ACT.Identity, bias=bias_shift[c][:])
+                unbiased = product(weights_shift, c, piece)
+                nc.scalar.activation(shift[c][:, columns], unbiased[:], ACT.Identity, bias=bias_shift[c])
 
         for c in range(BLOCKS):
             scaled = held.tile([P, N], F32, name=f"scaled{c}")

@@ -81,20 +81,15 @@ def tile_maskedcouplingaffine_kernel(
                     scale[c][:, columns], unclipped[:, columns], math.exp(LO), math.exp(HI), ALU.max, ALU.min
                 )
 
-        shift = []
-        for c in range(BLOCKS):
-            shift.append(held.tile([P, N], F32, name=f"shift{c}"))
-            for piece in range(PIECES):
-                columns = slice(piece * PIECE, (piece + 1) * PIECE)
-                unbiased = product(weights_shift, c, piece)
-                nc.scalar.activation(shift[c][:, columns], unbiased[:], ACT.Identity, bias=bias_shift[c])
-
         for c in range(BLOCKS):
             scaled = held.tile([P, N], F32, name=f"scaled{c}")
             result = held.tile([P, N], F32, name=f"result{c}")
+            shift = [product(weights_shift, c, piece) for piece in range(PIECES)]
             for piece in range(PIECES):
                 columns = slice(piece * PIECE, (piece + 1) * PIECE)
                 picked = store[c][:].indirect(offsets[:, piece * (PIECE // 16) : (piece + 1) * (PIECE // 16)])
                 nc.vector.tensor_tensor(scaled[:, columns], picked, scale[c][:, columns], ALU.mult)
-                nc.gpsimd.tensor_tensor(result[:, columns], scaled[:, columns], shift[c][:, columns], ALU.add)
+                nc.vector.scalar_tensor_tensor(
+                    result[:, columns], shift[piece][:], bias_shift[c], scaled[:, columns], ALU.add, ALU.add
+                )
                 nc.sync.dma_start(out[c * P : (c + 1) * P, columns], result[:, columns])

@@ -1,5 +1,3 @@
-import math
-
 import concourse.mybir as mybir
 
 F32 = mybir.dt.float32
@@ -25,7 +23,8 @@ def tile_maskedcouplingaffine_kernel(
     with (
         tc.tile_pool(name="held", bufs=1) as held,
         tc.psum_pool(name="psum_bias", bufs=1) as psum_bias,
-        tc.psum_pool(name="psum", bufs=7) as psum,
+        tc.psum_pool(name="psum_scale", bufs=2) as psum_scale,
+        tc.psum_pool(name="psum_shift", bufs=5) as psum_shift,
     ):
         bias_rows = held.tile([1, 2 * C], F32, name="bias_rows")
         nc.sync.dma_start(bias_rows[:, 0:C], b_scale.rearrange("c one -> one c"))
@@ -34,31 +33,35 @@ def tile_maskedcouplingaffine_kernel(
         nc.sync.dma_start(offsets[:], offs)
         weights_scale = held.tile([P, BLOCKS, C], BF16, name="weights_scale")
         nc.sync.dma_start(weights_scale[:], w_scale.rearrange("(k p) c -> p k c", p=P))
+        weights_shift = held.tile([P, BLOCKS, C], BF16, name="weights_shift")
+        nc.sync.dma_start(weights_shift[:], w_shift.rearrange("(k p) c -> p k c", p=P))
         masked = held.tile([P, BLOCKS, N], BF16, name="masked")
         masked_dram = x_masked.rearrange("(k p) n -> p k n", p=P)
         for half in range(2):
             columns = slice(half * (N // 2), (half + 1) * (N // 2))
             nc.sync.dma_start(masked[:, :, columns], masked_dram[:, :, columns])
-        store = [held.tile([P, S], F32, name=f"store{c}") for c in range(BLOCKS)]
-        nc.sync.dma_start(store[0][:], x_store[0:P, :])
-        weights_shift = held.tile([P, BLOCKS, C], BF16, name="weights_shift")
-        nc.sync.dma_start(weights_shift[:], w_shift.rearrange("(k p) c -> p k c", p=P))
-        nc.sync.dma_start(store[1][:], x_store[P : 2 * P, :])
+        store = []
+        for c in range(BLOCKS):
+            store.append(held.tile([P, S], F32, name=f"store{c}"))
+            nc.sync.dma_start(store[c][:], x_store[c * P : (c + 1) * P, :])
 
         one = held.tile([1, 1], F32, name="one")
         nc.vector.memset(one[:], 1.0)
+        scratch = held.tile([1, 1], F32, name="scratch")
+        nc.scalar.activation(scratch[:], one[:], ACT.Exp)
+
+        biases = held.tile([P, 2 * BLOCKS], F32, name="biases")
         bias_bank = psum_bias.tile([P, 2 * BLOCKS], F32, name="bias_bank")
         for i in range(2 * BLOCKS):
             nc.tensor.matmul(
                 bias_bank[:, i : i + 1], bias_rows[:, i * P : (i + 1) * P], one[:], start=True, stop=True
             )
-        biases = held.tile([P, 2 * BLOCKS], F32, name="biases")
         nc.vector.tensor_copy(biases[:], bias_bank[:])
-        bias_scale = [biases[:, c : c + 1] for c in range(BLOCKS)]
         bias_shift = [biases[:, BLOCKS + c : BLOCKS + c + 1] for c in range(BLOCKS)]
+        bias_scale_less_lo = held.tile([P, BLOCKS], F32, name="bias_scale_less_lo")
+        nc.vector.tensor_scalar_add(bias_scale_less_lo[:], biases[:, 0:BLOCKS], -LO)
 
-        def product(weights, c, piece):
-            bank = psum.tile([P, PIECE], F32, name="bank")
+        def product(bank, weights, c, piece):
             for k in range(BLOCKS):
                 nc.tensor.matmul(
                     bank[:],
@@ -67,29 +70,30 @@ def tile_maskedcouplingaffine_kernel(
                     start=(k == 0),
                     stop=(k == BLOCKS - 1),
                 )
-            return bank
-
-        scale = []
-        for c in range(BLOCKS):
-            unclipped = held.tile([P, N], F32, name=f"unclipped{c}")
-            scale.append(held.tile([P, N], F32, name=f"scale{c}"))
-            for piece in range(PIECES):
-                columns = slice(piece * PIECE, (piece + 1) * PIECE)
-                log_scale = product(weights_scale, c, piece)
-                nc.scalar.activation(unclipped[:, columns], log_scale[:], ACT.Exp, bias=bias_scale[c])
-                nc.vector.tensor_scalar(
-                    scale[c][:, columns], unclipped[:, columns], math.exp(LO), math.exp(HI), ALU.max, ALU.min
-                )
 
         for c in range(BLOCKS):
+            over_lo = held.tile([P, N], F32, name=f"over_lo{c}")
+            under_hi = held.tile([P, N], F32, name=f"under_hi{c}")
+            scale = held.tile([P, N], F32, name=f"scale{c}")
             scaled = held.tile([P, N], F32, name=f"scaled{c}")
             result = held.tile([P, N], F32, name=f"result{c}")
-            shift = [product(weights_shift, c, piece) for piece in range(PIECES)]
             for piece in range(PIECES):
                 columns = slice(piece * PIECE, (piece + 1) * PIECE)
+
+                log_scale = psum_scale.tile([P, PIECE], F32, name="log_scale")
+                product(log_scale, weights_scale, c, piece)
+                nc.scalar.activation(
+                    over_lo[:, columns], log_scale[:], ACT.Relu, bias=bias_scale_less_lo[:, c : c + 1]
+                )
+                nc.scalar.activation(under_hi[:, columns], over_lo[:, columns], ACT.Relu, bias=HI - LO, scale=-1.0)
+                nc.scalar.activation(scale[:, columns], under_hi[:, columns], ACT.Exp, bias=HI, scale=-1.0)
+
+                shift = psum_shift.tile([P, PIECE], F32, name="shift")
+                product(shift, weights_shift, c, piece)
+
                 picked = store[c][:].indirect(offsets[:, piece * (PIECE // 16) : (piece + 1) * (PIECE // 16)])
-                nc.vector.tensor_tensor(scaled[:, columns], picked, scale[c][:, columns], ALU.mult)
+                nc.vector.tensor_tensor(scaled[:, columns], picked, scale[:, columns], ALU.mult)
                 nc.vector.scalar_tensor_tensor(
-                    result[:, columns], shift[piece][:], bias_shift[c], scaled[:, columns], ALU.add, ALU.add
+                    result[:, columns], shift[:], bias_shift[c], scaled[:, columns], ALU.add, ALU.add
                 )
                 nc.sync.dma_start(out[c * P : (c + 1) * P, columns], result[:, columns])

@@ -1,3 +1,6 @@
+import math
+
+import concourse.masks as masks
 import concourse.mybir as mybir
 
 F32 = mybir.dt.float32
@@ -20,12 +23,7 @@ def tile_maskedcouplingaffine_kernel(
     tc, x_store, x_masked, w_scale, b_scale, w_shift, b_shift, offs, out
 ):
     nc = tc.nc
-    with (
-        tc.tile_pool(name="held", bufs=1) as held,
-        tc.psum_pool(name="psum_bias", bufs=1) as psum_bias,
-        tc.psum_pool(name="psum_scale", bufs=2) as psum_scale,
-        tc.psum_pool(name="psum_shift", bufs=5) as psum_shift,
-    ):
+    with tc.tile_pool(name="held", bufs=1) as held:
         bias_rows = held.tile([1, 2 * C], F32, name="bias_rows")
         nc.sync.dma_start(bias_rows[:, 0:C], b_scale.rearrange("c one -> one c"))
         nc.sync.dma_start(bias_rows[:, C : 2 * C], b_shift.rearrange("c one -> one c"))
@@ -45,55 +43,77 @@ def tile_maskedcouplingaffine_kernel(
             store.append(held.tile([P, S], F32, name=f"store{c}"))
             nc.sync.dma_start(store[c][:], x_store[c * P : (c + 1) * P, :])
 
+        identity = held.tile([P, P], F32, name="identity")
+        masks.make_identity(nc, identity[:])
         one = held.tile([1, 1], F32, name="one")
         nc.vector.memset(one[:], 1.0)
         scratch = held.tile([1, 1], F32, name="scratch")
         nc.scalar.activation(scratch[:], one[:], ACT.Exp)
 
         biases = held.tile([P, 2 * BLOCKS], F32, name="biases")
-        bias_bank = psum_bias.tile([P, 2 * BLOCKS], F32, name="bias_bank")
-        for i in range(2 * BLOCKS):
-            nc.tensor.matmul(
-                bias_bank[:, i : i + 1], bias_rows[:, i * P : (i + 1) * P], one[:], start=True, stop=True
-            )
-        nc.vector.tensor_copy(biases[:], bias_bank[:])
+        with tc.psum_pool(name="psum_bias", bufs=1) as psum_bias:
+            bias_bank = psum_bias.tile([P, 2 * BLOCKS], F32, name="bias_bank")
+            for i in range(2 * BLOCKS):
+                nc.tensor.matmul(
+                    bias_bank[:, i : i + 1], bias_rows[:, i * P : (i + 1) * P], one[:], start=True, stop=True
+                )
+            nc.vector.tensor_copy(biases[:], bias_bank[:])
+        bias_scale = [biases[:, c : c + 1] for c in range(BLOCKS)]
         bias_shift = [biases[:, BLOCKS + c : BLOCKS + c + 1] for c in range(BLOCKS)]
         bias_scale_less_lo = held.tile([P, BLOCKS], F32, name="bias_scale_less_lo")
         nc.vector.tensor_scalar_add(bias_scale_less_lo[:], biases[:, 0:BLOCKS], -LO)
 
-        def product(bank, weights, c, piece):
-            for k in range(BLOCKS):
-                nc.tensor.matmul(
-                    bank[:],
-                    weights[:, k, c * P : (c + 1) * P],
-                    masked[:, k, piece * PIECE : (piece + 1) * PIECE],
-                    start=(k == 0),
-                    stop=(k == BLOCKS - 1),
-                )
+        with tc.psum_pool(name="psum", bufs=8) as psum:
 
-        for c in range(BLOCKS):
-            over_lo = held.tile([P, N], F32, name=f"over_lo{c}")
-            under_hi = held.tile([P, N], F32, name=f"under_hi{c}")
-            scale = held.tile([P, N], F32, name=f"scale{c}")
-            scaled = held.tile([P, N], F32, name=f"scaled{c}")
-            result = held.tile([P, N], F32, name=f"result{c}")
+            def product(weights, c, piece, stop):
+                bank = psum.tile([P, PIECE], F32, name="bank")
+                for k in range(BLOCKS):
+                    nc.tensor.matmul(
+                        bank[:],
+                        weights[:, k, c * P : (c + 1) * P],
+                        masked[:, k, piece * PIECE : (piece + 1) * PIECE],
+                        start=(k == 0),
+                        stop=(stop and k == BLOCKS - 1),
+                    )
+                return bank
+
+            scale = [held.tile([P, N], F32, name=f"scale{c}") for c in range(BLOCKS)]
+
+            unclipped = held.tile([P, N], F32, name="unclipped")
             for piece in range(PIECES):
                 columns = slice(piece * PIECE, (piece + 1) * PIECE)
-
-                log_scale = psum_scale.tile([P, PIECE], F32, name="log_scale")
-                product(log_scale, weights_scale, c, piece)
-                nc.scalar.activation(
-                    over_lo[:, columns], log_scale[:], ACT.Relu, bias=bias_scale_less_lo[:, c : c + 1]
+                log_scale = product(weights_scale, 0, piece, stop=True)
+                nc.scalar.activation(unclipped[:, columns], log_scale[:], ACT.Exp, bias=bias_scale[0])
+                nc.vector.tensor_scalar(
+                    scale[0][:, columns], unclipped[:, columns], math.exp(LO), math.exp(HI), ALU.max, ALU.min
                 )
+
+            over_lo = held.tile([P, N], F32, name="over_lo")
+            under_hi = held.tile([P, N], F32, name="under_hi")
+            for piece in range(PIECES):
+                columns = slice(piece * PIECE, (piece + 1) * PIECE)
+                log_scale = product(weights_scale, 1, piece, stop=True)
+                nc.scalar.activation(over_lo[:, columns], log_scale[:], ACT.Relu, bias=bias_scale_less_lo[:, 1:2])
                 nc.scalar.activation(under_hi[:, columns], over_lo[:, columns], ACT.Relu, bias=HI - LO, scale=-1.0)
-                nc.scalar.activation(scale[:, columns], under_hi[:, columns], ACT.Exp, bias=HI, scale=-1.0)
+                nc.scalar.activation(scale[1][:, columns], under_hi[:, columns], ACT.Exp, bias=HI, scale=-1.0)
 
-                shift = psum_shift.tile([P, PIECE], F32, name="shift")
-                product(shift, weights_shift, c, piece)
+            shift = [
+                [product(weights_shift, c, piece, stop=(c == 1)) for piece in range(PIECES)] for c in range(BLOCKS)
+            ]
 
-                picked = store[c][:].indirect(offsets[:, piece * (PIECE // 16) : (piece + 1) * (PIECE // 16)])
-                nc.vector.tensor_tensor(scaled[:, columns], picked, scale[:, columns], ALU.mult)
-                nc.vector.scalar_tensor_tensor(
-                    result[:, columns], shift[:], bias_shift[c], scaled[:, columns], ALU.add, ALU.add
-                )
-                nc.sync.dma_start(out[c * P : (c + 1) * P, columns], result[:, columns])
+            for c in range(BLOCKS):
+                scaled = held.tile([P, N], F32, name=f"scaled{c}")
+                result = held.tile([P, N], F32, name=f"result{c}")
+                for piece in range(PIECES):
+                    columns = slice(piece * PIECE, (piece + 1) * PIECE)
+                    picked = store[c][:].indirect(offsets[:, piece * (PIECE // 16) : (piece + 1) * (PIECE // 16)])
+                    nc.vector.tensor_tensor(scaled[:, columns], picked, scale[c][:, columns], ALU.mult)
+                    if c == 0:
+                        nc.tensor.matmul(shift[c][piece][:], identity[:], scaled[:, columns], start=False, stop=True)
+                        nc.scalar.activation(result[:, columns], shift[c][piece][:], ACT.Identity, bias=bias_shift[c])
+                        nc.scalar.dma_start(out[c * P : (c + 1) * P, columns], result[:, columns])
+                    else:
+                        nc.vector.scalar_tensor_tensor(
+                            result[:, columns], shift[c][piece][:], bias_shift[c], scaled[:, columns], ALU.add, ALU.add
+                        )
+                        nc.sync.dma_start(out[c * P : (c + 1) * P, columns], result[:, columns])

@@ -24,9 +24,10 @@ def tile_maskedcouplingaffine_kernel(
 ):
     nc = tc.nc
     with tc.tile_pool(name="held", bufs=1) as held:
-        bias_rows = held.tile([1, 2 * C], F32, name="bias_rows")
-        nc.sync.dma_start(bias_rows[:, 0:C], b_scale.rearrange("c one -> one c"))
-        nc.sync.dma_start(bias_rows[:, C : 2 * C], b_shift.rearrange("c one -> one c"))
+        biases_scale = held.tile([P, BLOCKS], F32, name="biases_scale")
+        nc.scalar.dma_start(biases_scale[:], b_scale.rearrange("(c p) one -> p (c one)", p=P))
+        biases_shift = held.tile([P, BLOCKS], F32, name="biases_shift")
+        nc.scalar.dma_start(biases_shift[:], b_shift.rearrange("(c p) one -> p (c one)", p=P))
         offsets = held.tile([P, N // 16], U16, name="offsets")
         nc.sync.dma_start(offsets[:], offs)
         weights_scale = held.tile([P, BLOCKS, C], BF16, name="weights_scale")
@@ -50,18 +51,10 @@ def tile_maskedcouplingaffine_kernel(
         scratch = held.tile([1, 1], F32, name="scratch")
         nc.scalar.activation(scratch[:], one[:], ACT.Exp)
 
-        biases = held.tile([P, 2 * BLOCKS], F32, name="biases")
-        with tc.psum_pool(name="psum_bias", bufs=1) as psum_bias:
-            bias_bank = psum_bias.tile([P, 2 * BLOCKS], F32, name="bias_bank")
-            for i in range(2 * BLOCKS):
-                nc.tensor.matmul(
-                    bias_bank[:, i : i + 1], bias_rows[:, i * P : (i + 1) * P], one[:], start=True, stop=True
-                )
-            nc.vector.tensor_copy(biases[:], bias_bank[:])
-        bias_scale = [biases[:, c : c + 1] for c in range(BLOCKS)]
-        bias_shift = [biases[:, BLOCKS + c : BLOCKS + c + 1] for c in range(BLOCKS)]
+        bias_scale = [biases_scale[:, c : c + 1] for c in range(BLOCKS)]
+        bias_shift = [biases_shift[:, c : c + 1] for c in range(BLOCKS)]
         bias_scale_less_lo = held.tile([P, BLOCKS], F32, name="bias_scale_less_lo")
-        nc.vector.tensor_scalar_add(bias_scale_less_lo[:], biases[:, 0:BLOCKS], -LO)
+        nc.vector.tensor_scalar_add(bias_scale_less_lo[:], biases_scale[:], -LO)
 
         with tc.psum_pool(name="psum", bufs=8) as psum:
 

@@ -14,6 +14,9 @@ C, S, N = 256, 4096, 2048
 BLOCKS = C // P
 PIECE = 512
 PIECES = N // PIECE
+LOOKUP = 2 * PIECE
+LOOKUPS = N // LOOKUP
+VECTOR_ADDS = ((), (0, 2, 3))
 LO, HI = -5.0, 3.0
 
 FLOPS = 2 * 2 * C * C * N
@@ -28,17 +31,17 @@ def tile_maskedcouplingaffine_kernel(
         nc.scalar.dma_start(biases_scale[:], b_scale.rearrange("(c p) one -> p (c one)", p=P))
         biases_shift = held.tile([P, BLOCKS], F32, name="biases_shift")
         nc.scalar.dma_start(biases_shift[:], b_shift.rearrange("(c p) one -> p (c one)", p=P))
-        offsets = held.tile([P, N // 16], U16, name="offsets")
-        nc.sync.dma_start(offsets[:], offs)
         weights_scale = held.tile([P, BLOCKS, C], BF16, name="weights_scale")
         nc.sync.dma_start(weights_scale[:], w_scale.rearrange("(k p) c -> p k c", p=P))
-        weights_shift = held.tile([P, BLOCKS, C], BF16, name="weights_shift")
-        nc.sync.dma_start(weights_shift[:], w_shift.rearrange("(k p) c -> p k c", p=P))
         masked = held.tile([P, BLOCKS, N], BF16, name="masked")
         masked_dram = x_masked.rearrange("(k p) n -> p k n", p=P)
         for half in range(2):
             columns = slice(half * (N // 2), (half + 1) * (N // 2))
             nc.sync.dma_start(masked[:, :, columns], masked_dram[:, :, columns])
+        weights_shift = held.tile([P, BLOCKS, C], BF16, name="weights_shift")
+        nc.sync.dma_start(weights_shift[:], w_shift.rearrange("(k p) c -> p k c", p=P))
+        offsets = held.tile([P, N // 16], U16, name="offsets")
+        nc.sync.dma_start(offsets[:], offs)
         store = []
         for c in range(BLOCKS):
             store.append(held.tile([P, S], F32, name=f"store{c}"))
@@ -87,26 +90,35 @@ def tile_maskedcouplingaffine_kernel(
                 columns = slice(piece * PIECE, (piece + 1) * PIECE)
                 log_scale = product(weights_scale, 1, piece, stop=True)
                 nc.scalar.activation(over_lo[:, columns], log_scale[:], ACT.Relu, bias=bias_scale_less_lo[:, 1:2])
+            for piece in range(PIECES):
+                columns = slice(piece * PIECE, (piece + 1) * PIECE)
                 nc.scalar.activation(under_hi[:, columns], over_lo[:, columns], ACT.Relu, bias=HI - LO, scale=-1.0)
                 nc.scalar.activation(scale[1][:, columns], under_hi[:, columns], ACT.Exp, bias=HI, scale=-1.0)
 
             shift = [
-                [product(weights_shift, c, piece, stop=(c == 1)) for piece in range(PIECES)] for c in range(BLOCKS)
+                [product(weights_shift, c, piece, stop=(piece in VECTOR_ADDS[c])) for piece in range(PIECES)]
+                for c in range(BLOCKS)
             ]
 
             for c in range(BLOCKS):
                 scaled = held.tile([P, N], F32, name=f"scaled{c}")
                 result = held.tile([P, N], F32, name=f"result{c}")
-                for piece in range(PIECES):
-                    columns = slice(piece * PIECE, (piece + 1) * PIECE)
-                    picked = store[c][:].indirect(offsets[:, piece * (PIECE // 16) : (piece + 1) * (PIECE // 16)])
-                    nc.vector.tensor_tensor(scaled[:, columns], picked, scale[c][:, columns], ALU.mult)
-                    if c == 0:
-                        nc.tensor.matmul(shift[c][piece][:], identity[:], scaled[:, columns], start=False, stop=True)
-                        nc.scalar.activation(result[:, columns], shift[c][piece][:], ACT.Identity, bias=bias_shift[c])
-                        nc.scalar.dma_start(out[c * P : (c + 1) * P, columns], result[:, columns])
-                    else:
-                        nc.vector.scalar_tensor_tensor(
-                            result[:, columns], shift[c][piece][:], bias_shift[c], scaled[:, columns], ALU.add, ALU.add
-                        )
-                        nc.sync.dma_start(out[c * P : (c + 1) * P, columns], result[:, columns])
+                for lookup in range(LOOKUPS):
+                    wide = slice(lookup * LOOKUP, (lookup + 1) * LOOKUP)
+                    picked = store[c][:].indirect(offsets[:, lookup * (LOOKUP // 16) : (lookup + 1) * (LOOKUP // 16)])
+                    nc.vector.tensor_tensor(scaled[:, wide], picked, scale[c][:, wide], ALU.mult)
+                    for piece in range(lookup * (LOOKUP // PIECE), (lookup + 1) * (LOOKUP // PIECE)):
+                        columns = slice(piece * PIECE, (piece + 1) * PIECE)
+                        if piece in VECTOR_ADDS[c]:
+                            nc.vector.scalar_tensor_tensor(
+                                result[:, columns], shift[c][piece][:], bias_shift[c], scaled[:, columns], ALU.add, ALU.add
+                            )
+                            nc.sync.dma_start(out[c * P : (c + 1) * P, columns], result[:, columns])
+                        else:
+                            nc.tensor.matmul(
+                                shift[c][piece][:], identity[:], scaled[:, columns], start=False, stop=True
+                            )
+                            nc.scalar.activation(
+                                result[:, columns], shift[c][piece][:], ACT.Identity, bias=bias_shift[c]
+                            )
+                            nc.scalar.dma_start(out[c * P : (c + 1) * P, columns], result[:, columns])

@@ -95,15 +95,24 @@ def tile_maskedcouplingaffine_kernel(
                 nc.scalar.activation(under_hi[:, columns], over_lo[:, columns], ACT.Relu, bias=HI - LO, scale=-1.0)
                 nc.scalar.activation(scale[1][:, columns], under_hi[:, columns], ACT.Exp, bias=HI, scale=-1.0)
 
-            shift = [
-                [product(weights_shift, c, piece, stop=(piece in VECTOR_ADDS[c])) for piece in range(PIECES)]
-                for c in range(BLOCKS)
-            ]
+            shift = {}
+
+            def shift_products(c, lookup):
+                for piece in range(lookup * (LOOKUP // PIECE), (lookup + 1) * (LOOKUP // PIECE)):
+                    shift[c, piece] = product(weights_shift, c, piece, stop=(piece in VECTOR_ADDS[c]))
+
+            last = (BLOCKS - 1, LOOKUPS - 1)
+            for c in range(BLOCKS):
+                for lookup in range(LOOKUPS):
+                    if (c, lookup) != last:
+                        shift_products(c, lookup)
 
             for c in range(BLOCKS):
                 scaled = held.tile([P, N], F32, name=f"scaled{c}")
                 result = held.tile([P, N], F32, name=f"result{c}")
                 for lookup in range(LOOKUPS):
+                    if (c, lookup) == last:
+                        shift_products(c, lookup)
                     wide = slice(lookup * LOOKUP, (lookup + 1) * LOOKUP)
                     picked = store[c][:].indirect(offsets[:, lookup * (LOOKUP // 16) : (lookup + 1) * (LOOKUP // 16)])
                     nc.vector.tensor_tensor(scaled[:, wide], picked, scale[c][:, wide], ALU.mult)
@@ -111,14 +120,14 @@ def tile_maskedcouplingaffine_kernel(
                         columns = slice(piece * PIECE, (piece + 1) * PIECE)
                         if piece in VECTOR_ADDS[c]:
                             nc.vector.scalar_tensor_tensor(
-                                result[:, columns], shift[c][piece][:], bias_shift[c], scaled[:, columns], ALU.add, ALU.add
+                                result[:, columns], shift[c, piece][:], bias_shift[c], scaled[:, columns], ALU.add, ALU.add
                             )
                             nc.sync.dma_start(out[c * P : (c + 1) * P, columns], result[:, columns])
                         else:
                             nc.tensor.matmul(
-                                shift[c][piece][:], identity[:], scaled[:, columns], start=False, stop=True
+                                shift[c, piece][:], identity[:], scaled[:, columns], start=False, stop=True
                             )
                             nc.scalar.activation(
-                                result[:, columns], shift[c][piece][:], ACT.Identity, bias=bias_shift[c]
+                                result[:, columns], shift[c, piece][:], ACT.Identity, bias=bias_shift[c]
                             )
                             nc.scalar.dma_start(out[c * P : (c + 1) * P, columns], result[:, columns])

@@ -16,7 +16,9 @@ PIECE = 512
 PIECES = N // PIECE
 LOOKUP = 2 * PIECE
 LOOKUPS = N // LOOKUP
-VECTOR_ADDS = ((), (0, 2, 3))
+VECTOR_ADDS = ((), (1, 2, 3))
+BANKS = {"most": 6, "shared": 2}
+SHARED = ((0, 3), (1, 0), (1, 2), (1, 3))
 LO, HI = -5.0, 3.0
 
 FLOPS = 2 * 2 * C * C * N
@@ -59,10 +61,10 @@ def tile_maskedcouplingaffine_kernel(
         bias_scale_less_lo = held.tile([P, BLOCKS], F32, name="bias_scale_less_lo")
         nc.vector.tensor_scalar_add(bias_scale_less_lo[:], biases_scale[:], -LO)
 
-        with tc.psum_pool(name="psum", bufs=8) as psum:
+        with tc.psum_pool(name="psum", bufs=1) as psum:
 
-            def product(weights, c, piece, stop):
-                bank = psum.tile([P, PIECE], F32, name="bank")
+            def product(weights, c, piece, stop, tag):
+                bank = psum.tile([P, PIECE], F32, name="bank", tag=tag, bufs=BANKS[tag])
                 for k in range(BLOCKS):
                     nc.tensor.matmul(
                         bank[:],
@@ -78,7 +80,7 @@ def tile_maskedcouplingaffine_kernel(
             unclipped = held.tile([P, N], F32, name="unclipped")
             for piece in range(PIECES):
                 columns = slice(piece * PIECE, (piece + 1) * PIECE)
-                log_scale = product(weights_scale, 0, piece, stop=True)
+                log_scale = product(weights_scale, 0, piece, stop=True, tag="most")
                 nc.scalar.activation(unclipped[:, columns], log_scale[:], ACT.Exp, bias=bias_scale[0])
                 nc.vector.tensor_scalar(
                     scale[0][:, columns], unclipped[:, columns], math.exp(LO), math.exp(HI), ALU.max, ALU.min
@@ -88,7 +90,7 @@ def tile_maskedcouplingaffine_kernel(
             under_hi = held.tile([P, N], F32, name="under_hi")
             for piece in range(PIECES):
                 columns = slice(piece * PIECE, (piece + 1) * PIECE)
-                log_scale = product(weights_scale, 1, piece, stop=True)
+                log_scale = product(weights_scale, 1, piece, stop=True, tag="most")
                 nc.scalar.activation(over_lo[:, columns], log_scale[:], ACT.Relu, bias=bias_scale_less_lo[:, 1:2])
             for piece in range(PIECES):
                 columns = slice(piece * PIECE, (piece + 1) * PIECE)
@@ -99,7 +101,8 @@ def tile_maskedcouplingaffine_kernel(
 
             def shift_products(c, lookup):
                 for piece in range(lookup * (LOOKUP // PIECE), (lookup + 1) * (LOOKUP // PIECE)):
-                    shift[c, piece] = product(weights_shift, c, piece, stop=(piece in VECTOR_ADDS[c]))
+                    tag = "shared" if (c, piece) in SHARED else "most"
+                    shift[c, piece] = product(weights_shift, c, piece, stop=(piece in VECTOR_ADDS[c]), tag=tag)
 
             last = (BLOCKS - 1, LOOKUPS - 1)
             for c in range(BLOCKS):

@@ -34,14 +34,11 @@ def tile_maskedcouplingaffine_kernel(
         biases_shift = held.tile([P, BLOCKS], F32, name="biases_shift")
         nc.scalar.dma_start(biases_shift[:], b_shift.rearrange("(c p) one -> p (c one)", p=P))
         weights_scale = held.tile([P, BLOCKS, C], BF16, name="weights_scale")
-        nc.sync.dma_start(weights_scale[:], w_scale.rearrange("(k p) c -> p k c", p=P))
+        nc.sync.dma_start(weights_scale[:], w_scale.rearrange("(p r) c -> p r c", r=BLOCKS))
         masked = held.tile([P, BLOCKS, N], BF16, name="masked")
-        masked_dram = x_masked.rearrange("(k p) n -> p k n", p=P)
-        for half in range(2):
-            columns = slice(half * (N // 2), (half + 1) * (N // 2))
-            nc.sync.dma_start(masked[:, :, columns], masked_dram[:, :, columns])
+        nc.sync.dma_start(masked[:], x_masked.rearrange("(p r) n -> p r n", r=BLOCKS))
         weights_shift = held.tile([P, BLOCKS, C], BF16, name="weights_shift")
-        nc.sync.dma_start(weights_shift[:], w_shift.rearrange("(k p) c -> p k c", p=P))
+        nc.sync.dma_start(weights_shift[:], w_shift.rearrange("(p r) c -> p r c", r=BLOCKS))
         offsets = held.tile([P, N // 16], U16, name="offsets")
         nc.sync.dma_start(offsets[:], offs)
         store = []

@@ -30,9 +30,9 @@ def tile_maskedcouplingaffine_kernel(
     nc = tc.nc
     with tc.tile_pool(name="held", bufs=1) as held:
         biases_scale = held.tile([P, BLOCKS], F32, name="biases_scale")
-        nc.scalar.dma_start(biases_scale[:], b_scale.rearrange("(c p) one -> p (c one)", p=P))
+        nc.scalar.dma_start(biases_scale[:], b_scale.rearrange("(p b) one -> p (b one)", b=BLOCKS))
         biases_shift = held.tile([P, BLOCKS], F32, name="biases_shift")
-        nc.scalar.dma_start(biases_shift[:], b_shift.rearrange("(c p) one -> p (c one)", p=P))
+        nc.scalar.dma_start(biases_shift[:], b_shift.rearrange("(p b) one -> p (b one)", b=BLOCKS))
         weights_scale = held.tile([P, BLOCKS, C], BF16, name="weights_scale")
         nc.sync.dma_start(weights_scale[:], w_scale.rearrange("(p r) c -> p r c", r=BLOCKS))
         masked = held.tile([P, BLOCKS, N], BF16, name="masked")
@@ -41,10 +41,12 @@ def tile_maskedcouplingaffine_kernel(
         nc.sync.dma_start(weights_shift[:], w_shift.rearrange("(p r) c -> p r c", r=BLOCKS))
         offsets = held.tile([P, N // 16], U16, name="offsets")
         nc.sync.dma_start(offsets[:], offs)
+        x_store_blocks = x_store.rearrange("(p b) s -> b p s", b=BLOCKS)
+        out_blocks = out.rearrange("(p b) n -> b p n", b=BLOCKS)
         store = []
         for c in range(BLOCKS):
             store.append(held.tile([P, S], F32, name=f"store{c}"))
-            nc.sync.dma_start(store[c][:], x_store[c * P : (c + 1) * P, :])
+            nc.sync.dma_start(store[c][:], x_store_blocks[c])
 
         identity = held.tile([P, P], F32, name="identity")
         masks.make_identity(nc, identity[:])
@@ -65,7 +67,7 @@ def tile_maskedcouplingaffine_kernel(
                 for k in range(BLOCKS):
                     nc.tensor.matmul(
                         bank[:],
-                        weights[:, k, c * P : (c + 1) * P],
+                        weights[:, k, c:C:BLOCKS],
                         masked[:, k, piece * PIECE : (piece + 1) * PIECE],
                         start=(k == 0),
                         stop=(stop and k == BLOCKS - 1),
@@ -122,7 +124,7 @@ def tile_maskedcouplingaffine_kernel(
                             nc.vector.scalar_tensor_tensor(
                                 result[:, columns], shift[c, piece][:], bias_shift[c], scaled[:, columns], ALU.add, ALU.add
                             )
-                            nc.sync.dma_start(out[c * P : (c + 1) * P, columns], result[:, columns])
+                            nc.sync.dma_start(out_blocks[c][:, columns], result[:, columns])
                         else:
                             nc.tensor.matmul(
                                 shift[c, piece][:], identity[:], scaled[:, columns], start=False, stop=True
@@ -130,4 +132,4 @@ def tile_maskedcouplingaffine_kernel(
                             nc.scalar.activation(
                                 result[:, columns], shift[c, piece][:], ACT.Identity, bias=bias_shift[c]
                             )
-                            nc.scalar.dma_start(out[c * P : (c + 1) * P, columns], result[:, columns])
+                            nc.scalar.dma_start(out_blocks[c][:, columns], result[:, columns])

@@ -16,9 +16,10 @@ PIECE = 512
 PIECES = N // PIECE
 LOOKUP = 2 * PIECE
 LOOKUPS = N // LOOKUP
+HALF = N // 2
 VECTOR_ADDS = ((), (1, 2, 3))
 BANKS = {"most": 6, "shared": 2}
-SHARED = ((0, 3), (1, 0), (1, 2), (1, 3))
+SHARED = ((0, 2), (0, 3), (1, 2), (1, 3))
 LO, HI = -5.0, 3.0
 
 FLOPS = 2 * 2 * C * C * N
@@ -35,10 +36,11 @@ def tile_maskedcouplingaffine_kernel(
         nc.scalar.dma_start(biases_shift[:], b_shift.rearrange("(p b) one -> p (b one)", b=BLOCKS))
         weights_scale = held.tile([P, BLOCKS, C], BF16, name="weights_scale")
         nc.sync.dma_start(weights_scale[:], w_scale.rearrange("(p r) c -> p r c", r=BLOCKS))
-        masked = held.tile([P, BLOCKS, N], BF16, name="masked")
-        nc.sync.dma_start(masked[:], x_masked.rearrange("(p r) n -> p r n", r=BLOCKS))
-        weights_shift = held.tile([P, BLOCKS, C], BF16, name="weights_shift")
-        nc.sync.dma_start(weights_shift[:], w_shift.rearrange("(p r) c -> p r c", r=BLOCKS))
+        masked = []
+        for half in range(N // HALF):
+            masked.append(held.tile([P, BLOCKS, HALF], BF16, name=f"masked{half}"))
+            columns = slice(half * HALF, (half + 1) * HALF)
+            nc.sync.dma_start(masked[half][:], x_masked.rearrange("(p r) n -> p r n", r=BLOCKS)[:, :, columns])
         offsets = held.tile([P, N // 16], U16, name="offsets")
         nc.sync.dma_start(offsets[:], offs)
         x_store_blocks = x_store.rearrange("(p b) s -> b p s", b=BLOCKS)
@@ -47,6 +49,9 @@ def tile_maskedcouplingaffine_kernel(
         for c in range(BLOCKS):
             store.append(held.tile([P, S], F32, name=f"store{c}"))
             nc.sync.dma_start(store[c][:], x_store_blocks[c])
+            if c == 0:
+                weights_shift = held.tile([P, BLOCKS, C], BF16, name="weights_shift")
+                nc.sync.dma_start(weights_shift[:], w_shift.rearrange("(p r) c -> p r c", r=BLOCKS))
 
         identity = held.tile([P, P], F32, name="identity")
         masks.make_identity(nc, identity[:])
@@ -64,11 +69,12 @@ def tile_maskedcouplingaffine_kernel(
 
             def product(weights, c, piece, stop, tag):
                 bank = psum.tile([P, PIECE], F32, name="bank", tag=tag, bufs=BANKS[tag])
+                half, start = divmod(piece * PIECE, HALF)
                 for k in range(BLOCKS):
                     nc.tensor.matmul(
                         bank[:],
                         weights[:, k, c:C:BLOCKS],
-                        masked[:, k, piece * PIECE : (piece + 1) * PIECE],
+                        masked[half][:, k, start : start + PIECE],
                         start=(k == 0),
                         stop=(stop and k == BLOCKS - 1),
                     )
@@ -124,7 +130,8 @@ def tile_maskedcouplingaffine_kernel(
                             nc.vector.scalar_tensor_tensor(
                                 result[:, columns], shift[c, piece][:], bias_shift[c], scaled[:, columns], ALU.add, ALU.add
                             )
-                            nc.sync.dma_start(out_blocks[c][:, columns], result[:, columns])
+                            queue = nc.sync if piece % 2 else nc.scalar
+                            queue.dma_start(out_blocks[c][:, columns], result[:, columns])
                         else:
                             nc.tensor.matmul(
                                 shift[c, piece][:], identity[:], scaled[:, columns], start=False, stop=True

@@ -14,10 +14,8 @@ C, S, N = 256, 4096, 2048
 BLOCKS = C // P
 PIECE = 512
 PIECES = N // PIECE
-LOOKUP = 2 * PIECE
-LOOKUPS = N // LOOKUP
 HALF = N // 2
-VECTOR_ADDS = ((), (1, 2, 3))
+VECTOR_ADDS = ((1, 0), (1, 2), (1, 3))
 BANKS = {"most": 6, "shared": 2}
 SHARED = ((0, 2), (0, 3), (1, 2), (1, 3))
 LO, HI = -5.0, 3.0
@@ -104,39 +102,54 @@ def tile_maskedcouplingaffine_kernel(
 
             shift = {}
 
-            def shift_products(c, lookup):
-                for piece in range(lookup * (LOOKUP // PIECE), (lookup + 1) * (LOOKUP // PIECE)):
-                    tag = "shared" if (c, piece) in SHARED else "most"
-                    shift[c, piece] = product(weights_shift, c, piece, stop=(piece in VECTOR_ADDS[c]), tag=tag)
+            def shift_product(c, piece):
+                tag = "shared" if (c, piece) in SHARED else "most"
+                shift[c, piece] = product(weights_shift, c, piece, stop=((c, piece) in VECTOR_ADDS), tag=tag)
 
-            last = (BLOCKS - 1, LOOKUPS - 1)
-            for c in range(BLOCKS):
-                for lookup in range(LOOKUPS):
-                    if (c, lookup) != last:
-                        shift_products(c, lookup)
+            scaled = [held.tile([P, N], F32, name=f"scaled{c}") for c in range(BLOCKS)]
+            result = [held.tile([P, N], F32, name=f"result{c}") for c in range(BLOCKS)]
 
-            for c in range(BLOCKS):
-                scaled = held.tile([P, N], F32, name=f"scaled{c}")
-                result = held.tile([P, N], F32, name=f"result{c}")
-                for lookup in range(LOOKUPS):
-                    if (c, lookup) == last:
-                        shift_products(c, lookup)
-                    wide = slice(lookup * LOOKUP, (lookup + 1) * LOOKUP)
-                    picked = store[c][:].indirect(offsets[:, lookup * (LOOKUP // 16) : (lookup + 1) * (LOOKUP // 16)])
-                    nc.vector.tensor_tensor(scaled[:, wide], picked, scale[c][:, wide], ALU.mult)
-                    for piece in range(lookup * (LOOKUP // PIECE), (lookup + 1) * (LOOKUP // PIECE)):
-                        columns = slice(piece * PIECE, (piece + 1) * PIECE)
-                        if piece in VECTOR_ADDS[c]:
-                            nc.vector.scalar_tensor_tensor(
-                                result[:, columns], shift[c, piece][:], bias_shift[c], scaled[:, columns], ALU.add, ALU.add
-                            )
-                            queue = nc.sync if piece % 2 else nc.scalar
-                            queue.dma_start(out_blocks[c][:, columns], result[:, columns])
-                        else:
-                            nc.tensor.matmul(
-                                shift[c, piece][:], identity[:], scaled[:, columns], start=False, stop=True
-                            )
-                            nc.scalar.activation(
-                                result[:, columns], shift[c, piece][:], ACT.Identity, bias=bias_shift[c]
-                            )
-                            nc.scalar.dma_start(out_blocks[c][:, columns], result[:, columns])
+            def look_up(c, pieces):
+                first, end = pieces[0] * PIECE, (pieces[-1] + 1) * PIECE
+                picked = store[c][:].indirect(offsets[:, first // 16 : end // 16])
+                nc.vector.tensor_tensor(scaled[c][:, first:end], picked, scale[c][:, first:end], ALU.mult)
+
+            def add_shift(c, piece):
+                columns = slice(piece * PIECE, (piece + 1) * PIECE)
+                if (c, piece) in VECTOR_ADDS:
+                    halves = 2 if (c, piece) == (BLOCKS - 1, PIECES - 1) else 1
+                    width = PIECE // halves
+                    for part in range(halves):
+                        in_bank = slice(part * width, (part + 1) * width)
+                        columns = slice(piece * PIECE + part * width, piece * PIECE + (part + 1) * width)
+                        nc.vector.scalar_tensor_tensor(
+                            result[c][:, columns],
+                            shift[c, piece][:, in_bank],
+                            bias_shift[c],
+                            scaled[c][:, columns],
+                            ALU.add,
+                            ALU.add,
+                        )
+                        nc.sync.dma_start(out_blocks[c][:, columns], result[c][:, columns])
+                else:
+                    nc.tensor.matmul(shift[c, piece][:], identity[:], scaled[c][:, columns], start=False, stop=True)
+                    nc.scalar.activation(
+                        result[c][:, columns], shift[c, piece][:], ACT.Identity, bias=bias_shift[c]
+                    )
+                    nc.scalar.dma_start(out_blocks[c][:, columns], result[c][:, columns])
+
+            for c, piece in ((0, 0), (0, 1), (0, 2), (0, 3), (1, 0), (1, 1)):
+                shift_product(c, piece)
+            for pieces in ((0, 1), (2, 3)):
+                look_up(0, pieces)
+                for piece in pieces:
+                    add_shift(0, piece)
+            look_up(1, (0,))
+            look_up(1, (1,))
+            add_shift(1, 0)
+            add_shift(1, 1)
+            shift_product(1, 2)
+            shift_product(1, 3)
+            look_up(1, (2, 3))
+            add_shift(1, 2)
+            add_shift(1, 3)

@@ -117,7 +117,7 @@ def tile_maskedcouplingaffine_kernel(
             def add_shift(c, piece):
                 columns = slice(piece * PIECE, (piece + 1) * PIECE)
                 if (c, piece) in VECTOR_ADDS:
-                    halves = 2 if (c, piece) == (BLOCKS - 1, PIECES - 1) else 1
+                    halves = 2 if c == BLOCKS - 1 and piece >= PIECES - 2 else 1
                     width = PIECE // halves
                     for part in range(halves):
                         in_bank = slice(part * width, (part + 1) * width)

import math

import concourse.masks as masks
import concourse.mybir as mybir

F32 = mybir.dt.float32
BF16 = mybir.dt.bfloat16
U16 = mybir.dt.uint16
ALU = mybir.AluOpType
ACT = mybir.ActivationFunctionType

P = 128
C, S, N = 256, 4096, 2048
BLOCKS = C // P
PIECE = 512
PIECES = N // PIECE
HALF = N // 2
VECTOR_ADDS = ((1, 0), (1, 2), (1, 3))
BANKS = {"most": 6, "shared": 2}
SHARED = ((0, 2), (0, 3), (1, 2), (1, 3))
LO, HI = -5.0, 3.0

FLOPS = 2 * 2 * C * C * N


def tile_maskedcouplingaffine_kernel(
    tc, x_store, x_masked, w_scale, b_scale, w_shift, b_shift, offs, out
):
    nc = tc.nc
    with tc.tile_pool(name="held", bufs=1) as held:
        biases_scale = held.tile([P, BLOCKS], F32, name="biases_scale")
        nc.scalar.dma_start(biases_scale[:], b_scale.rearrange("(p b) one -> p (b one)", b=BLOCKS))
        biases_shift = held.tile([P, BLOCKS], F32, name="biases_shift")
        nc.scalar.dma_start(biases_shift[:], b_shift.rearrange("(p b) one -> p (b one)", b=BLOCKS))
        weights_scale = held.tile([P, BLOCKS, C], BF16, name="weights_scale")
        nc.sync.dma_start(weights_scale[:], w_scale.rearrange("(p r) c -> p r c", r=BLOCKS))
        masked = []
        for half in range(N // HALF):
            masked.append(held.tile([P, BLOCKS, HALF], BF16, name=f"masked{half}"))
            columns = slice(half * HALF, (half + 1) * HALF)
            nc.sync.dma_start(masked[half][:], x_masked.rearrange("(p r) n -> p r n", r=BLOCKS)[:, :, columns])
        offsets = held.tile([P, N // 16], U16, name="offsets")
        nc.sync.dma_start(offsets[:], offs)
        x_store_blocks = x_store.rearrange("(p b) s -> b p s", b=BLOCKS)
        out_blocks = out.rearrange("(p b) n -> b p n", b=BLOCKS)
        store = []
        for c in range(BLOCKS):
            store.append(held.tile([P, S], F32, name=f"store{c}"))
            nc.sync.dma_start(store[c][:], x_store_blocks[c])
            if c == 0:
                weights_shift = held.tile([P, BLOCKS, C], BF16, name="weights_shift")
                nc.sync.dma_start(weights_shift[:], w_shift.rearrange("(p r) c -> p r c", r=BLOCKS))

        identity = held.tile([P, P], F32, name="identity")
        masks.make_identity(nc, identity[:])
        one = held.tile([1, 1], F32, name="one")
        nc.vector.memset(one[:], 1.0)
        scratch = held.tile([1, 1], F32, name="scratch")
        nc.scalar.activation(scratch[:], one[:], ACT.Exp)

        bias_scale = [biases_scale[:, c : c + 1] for c in range(BLOCKS)]
        bias_shift = [biases_shift[:, c : c + 1] for c in range(BLOCKS)]
        bias_scale_less_lo = held.tile([P, BLOCKS], F32, name="bias_scale_less_lo")
        nc.vector.tensor_scalar_add(bias_scale_less_lo[:], biases_scale[:], -LO)

        with tc.psum_pool(name="psum", bufs=1) as psum:

            def product(weights, c, piece, stop, tag):
                bank = psum.tile([P, PIECE], F32, name="bank", tag=tag, bufs=BANKS[tag])
                half, start = divmod(piece * PIECE, HALF)
                for k in range(BLOCKS):
                    nc.tensor.matmul(
                        bank[:],
                        weights[:, k, c:C:BLOCKS],
                        masked[half][:, k, start : start + PIECE],
                        start=(k == 0),
                        stop=(stop and k == BLOCKS - 1),
                    )
                return bank

            scale = [held.tile([P, N], F32, name=f"scale{c}") for c in range(BLOCKS)]

            unclipped = held.tile([P, N], F32, name="unclipped")
            for piece in range(PIECES):
                columns = slice(piece * PIECE, (piece + 1) * PIECE)
                log_scale = product(weights_scale, 0, piece, stop=True, tag="most")
                nc.scalar.activation(unclipped[:, columns], log_scale[:], ACT.Exp, bias=bias_scale[0])
                nc.vector.tensor_scalar(
                    scale[0][:, columns], unclipped[:, columns], math.exp(LO), math.exp(HI), ALU.max, ALU.min
                )

            over_lo = held.tile([P, N], F32, name="over_lo")
            under_hi = held.tile([P, N], F32, name="under_hi")
            for piece in range(PIECES):
                columns = slice(piece * PIECE, (piece + 1) * PIECE)
                log_scale = product(weights_scale, 1, piece, stop=True, tag="most")
                nc.scalar.activation(over_lo[:, columns], log_scale[:], ACT.Relu, bias=bias_scale_less_lo[:, 1:2])
            for piece in range(PIECES):
                columns = slice(piece * PIECE, (piece + 1) * PIECE)
                nc.scalar.activation(under_hi[:, columns], over_lo[:, columns], ACT.Relu, bias=HI - LO, scale=-1.0)
                nc.scalar.activation(scale[1][:, columns], under_hi[:, columns], ACT.Exp, bias=HI, scale=-1.0)

            shift = {}

            def shift_product(c, piece):
                tag = "shared" if (c, piece) in SHARED else "most"
                shift[c, piece] = product(weights_shift, c, piece, stop=((c, piece) in VECTOR_ADDS), tag=tag)

            scaled = [held.tile([P, N], F32, name=f"scaled{c}") for c in range(BLOCKS)]
            result = [held.tile([P, N], F32, name=f"result{c}") for c in range(BLOCKS)]

            def look_up(c, pieces):
                first, end = pieces[0] * PIECE, (pieces[-1] + 1) * PIECE
                picked = store[c][:].indirect(offsets[:, first // 16 : end // 16])
                nc.vector.tensor_tensor(scaled[c][:, first:end], picked, scale[c][:, first:end], ALU.mult)

            def add_shift(c, piece):
                columns = slice(piece * PIECE, (piece + 1) * PIECE)
                if (c, piece) in VECTOR_ADDS:
                    halves = 2 if c == BLOCKS - 1 and piece >= PIECES - 2 else 1
                    width = PIECE // halves
                    for part in range(halves):
                        in_bank = slice(part * width, (part + 1) * width)
                        columns = slice(piece * PIECE + part * width, piece * PIECE + (part + 1) * width)
                        nc.vector.scalar_tensor_tensor(
                            result[c][:, columns],
                            shift[c, piece][:, in_bank],
                            bias_shift[c],
                            scaled[c][:, columns],
                            ALU.add,
                            ALU.add,
                        )
                        nc.sync.dma_start(out_blocks[c][:, columns], result[c][:, columns])
                else:
                    nc.tensor.matmul(shift[c, piece][:], identity[:], scaled[c][:, columns], start=False, stop=True)
                    nc.scalar.activation(
                        result[c][:, columns], shift[c, piece][:], ACT.Identity, bias=bias_shift[c]
                    )
                    nc.scalar.dma_start(out_blocks[c][:, columns], result[c][:, columns])

            for c, piece in ((0, 0), (0, 1), (0, 2), (0, 3), (1, 0), (1, 1)):
                shift_product(c, piece)
            for pieces in ((0, 1), (2, 3)):
                look_up(0, pieces)
                for piece in pieces:
                    add_shift(0, piece)
            look_up(1, (0,))
            look_up(1, (1,))
            add_shift(1, 0)
            add_shift(1, 1)
            shift_product(1, 2)
            shift_product(1, 3)
            look_up(1, (2, 3))
            add_shift(1, 2)
            add_shift(1, 3)
